import numpy as np
import ml_dtypes


def mxq(x, axis, fmt="e4m3"):
    dtype, down = {"e4m3": (ml_dtypes.float8_e4m3fn, 7), "e5m2": (ml_dtypes.float8_e5m2, 14)}[fmt]
    v = np.moveaxis(np.asarray(x, np.float32).astype(ml_dtypes.bfloat16).astype(np.float64), axis, -1)
    blocks = v.reshape(v.shape[:-1] + (-1, 32))
    amax = np.abs(blocks).max(-1, keepdims=True)
    byte = np.maximum(np.where(amax > 0, np.frexp(amax)[1] - 1 + 127, 0) - down, 1)
    scale = np.exp2(byte - 127.0)
    codes = (blocks / scale).astype(np.float32).astype(dtype).astype(np.float64)
    return np.moveaxis((codes * scale).reshape(v.shape), -1, axis)


WIDE = False


def mx_kscale(k):
    if not WIDE:
        return np.ones(k)
    levels = np.array([10, -10, 5, -5, 0])
    a = np.random.permutation(np.resize(levels, k // 512 * 4)).reshape(k // 512, 4)
    idx = np.arange(k)
    return np.exp2(a[idx // 512, idx % 128 // 32])


BF16 = ml_dtypes.bfloat16


def bf(x):
    return np.asarray(x, np.float32).astype(BF16)


def f64(x):
    return np.asarray(x).astype(np.float64)


E2M1 = np.array([0.0, 0.5, 1.0, 1.5, 2.0, 3.0, 4.0, 6.0, -0.0, -0.5, -1.0, -1.5, -2.0, -3.0, -4.0, -6.0])


def pack_weight(w, fmt):
    k, n = w.shape
    w = f64(bf(w)).reshape(k // 32, 32, n)
    amax = np.abs(w).max(1)
    if fmt == "e4m3":
        byte = np.frexp(amax)[1] - 1 + 127 - 7
    else:
        mant, ex = np.frexp(amax / 6.0)
        byte = np.where(mant > 0.5, ex, ex - 1) + 127
    byte = np.clip(np.where(amax > 0, byte, 1), 1, 254)
    scaled = (w * np.exp2(127.0 - byte)[:, None, :]).reshape(k, n).astype(np.float32)
    by_word = np.ascontiguousarray(scaled.reshape(k // 512, 128, 4, n).transpose(0, 1, 3, 2))
    if fmt == "e4m3":
        words = by_word.astype(ml_dtypes.float8_e4m3fn).view(np.uint8)
    else:
        c = by_word.astype(ml_dtypes.float4_e2m1fn).view(np.uint8) & 0xF
        words = c[..., 0::2] | (c[..., 1::2] << 4)
    return np.ascontiguousarray(words), np.ascontiguousarray(byte.astype(np.uint8).reshape(k // 512, 16, n))


def unpack_weight(words, scales, fmt):
    g, p, n, _ = words.shape
    if fmt == "e4m3":
        vals = np.ascontiguousarray(words).view(ml_dtypes.float8_e4m3fn).astype(np.float64)
    else:
        nib = np.empty((g, p, n, 4), np.uint8)
        nib[..., 0::2] = words & 0xF
        nib[..., 1::2] = words >> 4
        vals = E2M1[nib]
    vals = vals * np.repeat(np.exp2(scales.astype(np.float64) - 127.0), 8, axis=1)[..., None]
    return vals.transpose(0, 1, 3, 2).reshape(g * 512, n)


B, DH, DO, L = 128, 2048, 2048, 128


def setup_inputs():
    s = mx_kscale(2 * DH)
    t = mx_kscale(DO)
    sbj_vec = bf(np.random.standard_normal((B, DH)) * s[:DH])
    obj_vec = bf(np.random.standard_normal((B, DH)) * s[DH:])
    W1_words, W1_scales = pack_weight(np.random.standard_normal((2 * DH, DO)) * 1.28 / np.sqrt(2 * DH) / s[:, None] * t, "e4m3")
    b1 = bf(np.random.standard_normal(DO) * 0.1 * t)
    W2_words, W2_scales = pack_weight(np.random.standard_normal((DO, DO)) * 12.0 / DO / t[:, None], "e4m3")
    b2 = bf(np.random.standard_normal(DO) * 0.1)
    label_vecs = bf(np.random.standard_normal((L, DO)) * 8.0 / np.sqrt(DO))
    return {"sbj_vec": sbj_vec,
            "obj_vec": obj_vec,
            "W1_words": W1_words,
            "W1_scales": W1_scales,
            "b1": b1,
            "W2_words": W2_words,
            "W2_scales": W2_scales,
            "b2": b2,
            "label_vecs": label_vecs}


def reference(sbj_vec, obj_vec, W1_words, W1_scales, b1, W2_words, W2_scales, b2, label_vecs):
    x = np.concatenate([f64(sbj_vec), f64(obj_vec)], axis=1)
    hidden = (mxq(np.maximum(x, 0.0), 1, "e4m3") @ unpack_weight(W1_words, W1_scales, "e4m3")) + f64(b1)
    emb = (mxq(np.maximum(hidden, 0.0), 1, "e4m3") @ unpack_weight(W2_words, W2_scales, "e4m3")) + f64(b2)
    lab = f64(label_vecs)
    scores = np.empty((emb.shape[0], lab.shape[0]))
    for l in range(lab.shape[0]):
        diff = np.maximum(lab[l][None, :] - emb, 0.0)
        scores[:, l] = -np.sqrt(np.sum(diff * diff, axis=1))
    return scores

@@ -1,0 +1,256 @@
+from contextlib import ExitStack
+
+import concourse.mybir as mybir
+from concourse.masks import make_identity
+
+F32 = mybir.dt.float32
+BF16 = mybir.dt.bfloat16
+I32 = mybir.dt.int32
+U32 = mybir.dt.uint32
+U8 = mybir.dt.uint8
+FP8X4 = mybir.dt.float8_e4m3fn_x4
+ALU = mybir.AluOpType
+ACT = mybir.ActivationFunctionType
+AX = mybir.AxisListType
+
+P = 128
+B = 128
+L = 128
+DH = 2048
+DO = 2048
+G1 = 8
+G2 = 4
+NCG = 4
+VPER = 5
+NV = 25
+LAG = 3
+
+FLOPS = 2 * B * (2 * DH) * DO + 2 * B * DO * DO
+
+
+def tile_relationembedding_w_kernel(
+    tc, sbj_vec, obj_vec, W1_words, W1_scales, b1, W2_words, W2_scales, b2, label_vecs, out
+):
+    nc = tc.nc
+    with ExitStack() as ctx:
+        ctx.enter_context(tc.manual_schedule())
+        keep = ctx.enter_context(tc.tile_pool(name="keep", bufs=1))
+        rpool = ctx.enter_context(tc.tile_pool(name="rpool", bufs=6))
+        jpool = ctx.enter_context(tc.tile_pool(name="jpool", bufs=2))
+        psum = ctx.enter_context(tc.psum_pool(name="psum", bufs=8))
+
+        def bank(name, shape=(P, 512), dtype=F32):
+            return psum.tile(list(shape), dtype, name=name, tag="bank")
+
+        ident_f = keep.tile([P, P], F32, name="ident_f")
+        ident_b = keep.tile([P, P], BF16, name="ident_b")
+        make_identity(nc, ident_f[:])
+        make_identity(nc, ident_b[:])
+
+        planes = [keep.tile([P, 2048], U8, name="planes%d" % i, align_bytes=64) for i in range(3)]
+        for pl in planes:
+            nc.vector.memset(pl[:].bitcast(I32), 0)
+        zt = keep.tile([P, P], BF16, name="zt")
+        nc.vector.memset(zt[:], 0.0)
+        one = keep.tile([P, 1], F32, name="one")
+        nc.vector.memset(one[:], 1.0)
+        acc_s = keep.tile([P, NCG, L], F32, name="acc_s")
+        nc.vector.memset(acc_s[:], 0.0)
+        one2 = keep.tile([P, 1], F32, name="one2")
+        nc.scalar.activation(out=one2[:], in_=one[:], func=ACT.Sqrt)
+
+        x_sb = keep.tile([P, 2 * DH], BF16, name="x_sb")
+        nc.sync.dma_start(out=x_sb[:, 0:DH], in_=sbj_vec[:, :])
+        nc.sync.dma_start(out=x_sb[:, DH : 2 * DH], in_=obj_vec[:, :])
+        lab_sb = keep.tile([P, DO], BF16, name="lab_sb")
+        nc.sync.dma_start(out=lab_sb[:], in_=label_vecs[:, :])
+        nc.sync.dma_start(out=zt[0:16, :], in_=b2.rearrange("(c p) -> c p", p=P))
+        b1b = keep.tile([P, DO], BF16, name="b1b")
+        nc.sync.dma_start(out=b1b[:], in_=b1.partition_broadcast(P))
+        for i, src in ((0, W1_scales[0:4]), (1, W1_scales[4:8]), (2, W2_scales)):
+            for q in range(4):
+                nc.sync.dma_start(
+                    out=planes[i][32 * q : 32 * q + 16, :].bitcast(I32),
+                    in_=src[:, 4 * q : 4 * q + 4, :].bitcast(I32),
+                )
+        w1 = []
+        for g in range(G1):
+            w = keep.tile([P, DO], U32, name="w1_%d" % g, align_bytes=64)
+            nc.sync.dma_start(
+                out=w[:].bitcast(I32), in_=W1_words[g].rearrange("p n t -> p (n t)").bitcast(I32)
+            )
+            w1.append(w)
+        w2 = []
+        w2_view = W2_words.rearrange("g p n t -> p g (n t)")
+        for cg in range(NCG):
+            w = keep.tile([P, G2, 512], U32, name="w2_%d" % cg, align_bytes=64)
+            nc.sync.dma_start(
+                out=w[:].bitcast(I32), in_=w2_view[:, :, 2048 * cg : 2048 * (cg + 1)].bitcast(I32)
+            )
+            w2.append(w)
+
+        gx = keep.tile([P, G1, B, 4], BF16, name="gx", align_bytes=64)
+        xq = keep.tile([P, G1, B], U32, name="xq", align_bytes=64)
+        xs = keep.tile([P, G1, B], U8, name="xs", align_bytes=64)
+        for h in range(2):
+            nc.vector.tensor_scalar_max(
+                out=x_sb[:, DH * h : DH * (h + 1)], in0=x_sb[:, DH * h : DH * (h + 1)], scalar1=0.0
+            )
+        x_words = x_sb[:].bitcast(F32)
+        gx_words = gx[:].bitcast(F32)
+        for i in range(4):
+            xt = bank("xt%d" % i, (P, 2, 2, B))
+            for gg in range(2):
+                g = 2 * i + gg
+                for u in range(2):
+                    nc.tensor.transpose(
+                        xt[:, gg, u, :], x_words[:, 256 * g + u : 256 * (g + 1) : 2], ident_f[:]
+                    )
+            src = xt[:].rearrange("p g u b -> p g b u")
+            if i % 2 == 0:
+                nc.vector.tensor_copy(out=gx_words[:, 2 * i : 2 * i + 2], in_=src)
+            else:
+                nc.scalar.copy(out=gx_words[:, 2 * i : 2 * i + 2], in_=src)
+
+        lab_t = keep.tile([P, 16, L], F32, name="lab_t")
+        for i in range(2):
+            lp = bank("lp%d" % i, (P, 8, L), BF16)
+            for cc in range(8):
+                c = 8 * i + cc
+                nc.tensor.transpose(lp[:, cc, :], lab_sb[:, P * c : P * (c + 1)], ident_b[:])
+            if i == 0:
+                nc.scalar.copy(out=lab_t[:, 0:8, :], in_=lp[:])
+            else:
+                nc.vector.tensor_copy(out=lab_t[:, 8:16, :], in_=lp[:])
+        bp = bank("bp", (P, 1024), BF16)
+        nc.tensor.transpose(bp[:, 0:P], zt[:], ident_b[:])
+        b2_t = keep.tile([P, 16], F32, name="b2_t")
+        nc.vector.tensor_copy(out=b2_t[:], in_=bp[:, 0:16])
+
+        for h in range(2):
+            nc.vector.quantize_mx(
+                out=xq[:, 4 * h : 4 * h + 4, :].rearrange("p g b -> p (g b)").bitcast(FP8X4),
+                scales=xs[:, 4 * h : 4 * h + 4, :].rearrange("p g b -> p (g b)"),
+                in_=gx[:, 4 * h : 4 * h + 4].rearrange("p g b t -> p (g b t)"),
+            )
+
+        acc = [bank("acc%d" % nb) for nb in range(4)]
+        for g in range(G1):
+            k = 4 * (g % 4)
+            pl = planes[g // 4]
+            for nb in range(4):
+                cols = slice(512 * nb, 512 * (nb + 1))
+                nc.tensor.matmul_mx(
+                    out=acc[nb][:],
+                    lhsT=xq[:, g, :].bitcast(FP8X4),
+                    lhsT_scale=xs[:, g, :],
+                    rhs=w1[g][:, cols].bitcast(FP8X4),
+                    rhs_scale=pl[k:P, cols],
+                    start=(g == 0),
+                    stop=(g == G1 - 1),
+                )
+
+        h32 = keep.tile([P, DO], F32, name="h32")
+        hb = keep.tile([P, DO], BF16, name="hb")
+        gh = keep.tile([P, G2, B, 4], BF16, name="gh", align_bytes=64)
+        hq = keep.tile([P, G2, B], U32, name="hq", align_bytes=64)
+        hs = keep.tile([P, G2, B], U8, name="hs", align_bytes=64)
+        for g in range(G2):
+            cols = slice(512 * g, 512 * (g + 1))
+            nc.vector.tensor_tensor(out=h32[:, cols], in0=acc[g][:], in1=b1b[:, cols], op=ALU.add)
+            nc.scalar.activation(out=hb[:, cols], in_=h32[:, cols], func=ACT.Relu)
+        for g in range(G2):
+            ht = bank("ht%d" % g, (P, 8, B), BF16)
+            for t in range(4):
+                nc.tensor.transpose(ht[:, t, :], hb[:, 512 * g + t : 512 * (g + 1) : 4], ident_b[:])
+            src = ht[:, 0:4, :].rearrange("p t b -> p b t")
+            if g % 2 == 0:
+                nc.vector.tensor_copy(out=gh[:, g], in_=src)
+            else:
+                nc.scalar.copy(out=gh[:, g], in_=src)
+        nc.vector.quantize_mx(
+            out=hq[:].rearrange("p g b -> p (g b)").bitcast(FP8X4),
+            scales=hs[:].rearrange("p g b -> p (g b)"),
+            in_=gh[:].rearrange("p g b t -> p (g b t)"),
+        )
+
+        emb = [keep.tile([P, 4, B], F32, name="emb%d" % cg) for cg in range(NCG)]
+
+        def layer2(cg):
+            ep = bank("ep%d" % cg)
+            for j in range(4):
+                cols = slice(P * j, P * (j + 1))
+                for g in range(G2):
+                    nc.tensor.matmul_mx(
+                        out=ep[:, cols],
+                        lhsT=w2[cg][:, g, cols].bitcast(FP8X4),
+                        lhsT_scale=planes[2][4 * g : P, 512 * cg + P * j : 512 * cg + P * (j + 1)],
+                        rhs=hq[:, g, :].bitcast(FP8X4),
+                        rhs_scale=hs[:, g, :],
+                        start=(g == 0),
+                        stop=(g == G2 - 1),
+                    )
+            for j in range(4):
+                c = 4 * cg + j
+                nc.scalar.activation(
+                    out=emb[cg][:, j, :],
+                    in_=ep[:, P * j : P * (j + 1)],
+                    func=ACT.Identity,
+                    bias=b2_t[:, c : c + 1],
+                    scale=1.0,
+                )
+
+        stats = keep.tile([P, NCG, NV, 6], F32, name="stats")
+        pending = []
+
+        def sum_squares(cg, l, tp):
+            if l % VPER == VPER - 1:
+                nc.vector.bn_stats(out=stats[:, cg, l // VPER, :], in_=tp[:])
+            else:
+                junk = jpool.tile([P, 512], F32, name="junk", tag="junk")
+                nc.scalar.activation(
+                    out=junk[:], in_=tp[:], func=ACT.Square, accum_out=acc_s[:, cg, l : l + 1]
+                )
+
+        layer2(0)
+        for cg in range(NCG):
+            for l in range(L):
+                r = rpool.tile([P, 4, B], F32, name="r", tag="r")
+                for j in range(4):
+                    nc.vector.tensor_scalar(
+                        out=r[:, j, :],
+                        in0=emb[cg][:, j, :],
+                        scalar1=lab_t[:, 4 * cg + j, l : l + 1],
+                        scalar2=0.0,
+                        op0=ALU.subtract,
+                        op1=ALU.min,
+                    )
+                tp = bank("tp")
+                for j in range(4):
+                    nc.tensor.transpose(tp[:, P * j : P * (j + 1)], r[:, j, :], ident_f[:])
+                pending.append((cg, l, tp))
+                if len(pending) > LAG:
+                    sum_squares(*pending.pop(0))
+                if l == 64 and cg + 1 < NCG:
+                    layer2(cg + 1)
+        for item in pending:
+            sum_squares(*item)
+
+        tot = keep.tile([P, L], F32, name="tot")
+        nc.vector.tensor_reduce(out=tot[:], in_=acc_s[:].rearrange("p c l -> p l c"), axis=AX.X, op=ALU.add)
+        st = stats[:].rearrange("p c v (e s) -> p c v e s", s=3)
+        msq = keep.tile([P, NCG, NV, 2], F32, name="msq")
+        nc.vector.tensor_tensor(out=msq[:], in0=st[:, :, :, :, 1], in1=st[:, :, :, :, 1], op=ALU.mult)
+        ssq = keep.tile([P, NCG, NV, 2], F32, name="ssq")
+        nc.vector.scalar_tensor_tensor(
+            out=ssq[:], in0=msq[:], scalar=256.0, in1=st[:, :, :, :, 2], op0=ALU.mult, op1=ALU.add
+        )
+        sum_v = keep.tile([P, NV], F32, name="sum_v")
+        nc.vector.tensor_reduce(out=sum_v[:], in_=ssq[:].rearrange("p c v e -> p v c e"), axis=AX.XY, op=ALU.add)
+        tot_v = tot[:, 0 : VPER * NV].rearrange("p (v f) -> p v f", f=VPER)[:, :, VPER - 1]
+        nc.vector.tensor_tensor(out=tot_v, in0=tot_v, in1=sum_v[:], op=ALU.add)
+        root = keep.tile([P, L], F32, name="root")
+        nc.scalar.activation(out=root[:], in_=tot[:], func=ACT.Sqrt)
+        res = keep.tile([P, L], F32, name="res")
+        nc.vector.tensor_scalar_mul(out=res[:], in0=root[:], scalar1=-1.0)
+        nc.sync.dma_start(out=out[:, :], in_=res[:])

@@ -21,9 +21,9 @@ DO = 2048
 G1 = 8
 G2 = 4
 NCG = 4
-VPER = 5
-NV = 25
-LAG = 3
+NC = 16
+VC = 2
+LAG = 1
 
 FLOPS = 2 * B * (2 * DH) * DO + 2 * B * DO * DO
 
@@ -35,8 +35,7 @@ def tile_relationembedding_w_kernel(
     with ExitStack() as ctx:
         ctx.enter_context(tc.manual_schedule())
         keep = ctx.enter_context(tc.tile_pool(name="keep", bufs=1))
-        rpool = ctx.enter_context(tc.tile_pool(name="rpool", bufs=6))
-        jpool = ctx.enter_context(tc.tile_pool(name="jpool", bufs=2))
+        rpool = ctx.enter_context(tc.tile_pool(name="rpool", bufs=4))
         psum = ctx.enter_context(tc.psum_pool(name="psum", bufs=8))
 
         def bank(name, shape=(P, 512), dtype=F32):
@@ -54,8 +53,6 @@ def tile_relationembedding_w_kernel(
         nc.vector.memset(zt[:], 0.0)
         one = keep.tile([P, 1], F32, name="one")
         nc.vector.memset(one[:], 1.0)
-        acc_s = keep.tile([P, NCG, L], F32, name="acc_s")
-        nc.vector.memset(acc_s[:], 0.0)
         one2 = keep.tile([P, 1], F32, name="one2")
         nc.scalar.activation(out=one2[:], in_=one[:], func=ACT.Sqrt)
 
@@ -200,55 +197,54 @@ def tile_relationembedding_w_kernel(
                     scale=1.0,
                 )
 
-        stats = keep.tile([P, NCG, NV, 6], F32, name="stats")
-        pending = []
-
-        def sum_squares(cg, l, tp):
-            if l % VPER == VPER - 1:
-                nc.vector.bn_stats(out=stats[:, cg, l // VPER, :], in_=tp[:])
-            else:
-                junk = jpool.tile([P, 512], F32, name="junk", tag="junk")
-                nc.scalar.activation(
-                    out=junk[:], in_=tp[:], func=ACT.Square, accum_out=acc_s[:, cg, l : l + 1]
-                )
-
-        layer2(0)
         for cg in range(NCG):
-            for l in range(L):
-                r = rpool.tile([P, 4, B], F32, name="r", tag="r")
-                for j in range(4):
-                    nc.vector.tensor_scalar(
-                        out=r[:, j, :],
-                        in0=emb[cg][:, j, :],
-                        scalar1=lab_t[:, 4 * cg + j, l : l + 1],
-                        scalar2=0.0,
-                        op0=ALU.subtract,
-                        op1=ALU.min,
-                    )
-                tp = bank("tp")
-                for j in range(4):
-                    nc.tensor.transpose(tp[:, P * j : P * (j + 1)], r[:, j, :], ident_f[:])
-                pending.append((cg, l, tp))
-                if len(pending) > LAG:
-                    sum_squares(*pending.pop(0))
-                if l == 64 and cg + 1 < NCG:
-                    layer2(cg + 1)
-        for item in pending:
-            sum_squares(*item)
+            layer2(cg)
 
         tot = keep.tile([P, L], F32, name="tot")
-        nc.vector.tensor_reduce(out=tot[:], in_=acc_s[:].rearrange("p c l -> p l c"), axis=AX.X, op=ALU.add)
-        st = stats[:].rearrange("p c v (e s) -> p c v e s", s=3)
-        msq = keep.tile([P, NCG, NV, 2], F32, name="msq")
-        nc.vector.tensor_tensor(out=msq[:], in0=st[:, :, :, :, 1], in1=st[:, :, :, :, 1], op=ALU.mult)
-        ssq = keep.tile([P, NCG, NV, 2], F32, name="ssq")
-        nc.vector.scalar_tensor_tensor(
-            out=ssq[:], in0=msq[:], scalar=256.0, in1=st[:, :, :, :, 2], op0=ALU.mult, op1=ALU.add
-        )
-        sum_v = keep.tile([P, NV], F32, name="sum_v")
-        nc.vector.tensor_reduce(out=sum_v[:], in_=ssq[:].rearrange("p c v e -> p v c e"), axis=AX.XY, op=ALU.add)
-        tot_v = tot[:, 0 : VPER * NV].rearrange("p (v f) -> p v f", f=VPER)[:, :, VPER - 1]
-        nc.vector.tensor_tensor(out=tot_v, in0=tot_v, in1=sum_v[:], op=ALU.add)
+        pending = []
+
+        def reduce_bank(k, tp):
+            nc.vector.tensor_reduce(
+                out=tot[:, 4 * k : 4 * k + 4],
+                in_=tp[:].rearrange("p (l d) -> p l d", d=P),
+                axis=AX.X,
+                op=ALU.add,
+            )
+
+        mid = (VC + NC) // 2
+        tp = None
+        for l in range(L):
+            r = rpool.tile([P, NC, B], F32, name="r", tag="r")
+            for c in range(NC):
+                nc.vector.tensor_scalar(
+                    out=r[:, c, :],
+                    in0=emb[c // 4][:, c % 4, :],
+                    scalar1=lab_t[:, c, l : l + 1],
+                    scalar2=0.0,
+                    op0=ALU.subtract,
+                    op1=ALU.min,
+                )
+            nc.vector.tensor_tensor(out=r[:, 0:VC, :], in0=r[:, 0:VC, :], in1=r[:, 0:VC, :], op=ALU.mult)
+            nc.scalar.activation(out=r[:, VC:mid, :], in_=r[:, VC:mid, :], func=ACT.Square)
+            nc.scalar.activation(out=r[:, mid:NC, :], in_=r[:, mid:NC, :], func=ACT.Square)
+            if l % 4 == 0:
+                tp = bank("tp")
+            for c in range(NC):
+                nc.tensor.matmul(
+                    out=tp[:, P * (l % 4) : P * (l % 4 + 1)],
+                    lhsT=r[:, c, :],
+                    rhs=ident_f[:],
+                    is_transpose=True,
+                    start=(c == 0),
+                    stop=(c == NC - 1),
+                )
+            if l % 4 == 3:
+                pending.append((l // 4, tp))
+                if len(pending) > LAG:
+                    reduce_bank(*pending.pop(0))
+        for item in pending:
+            reduce_bank(*item)
+
         root = keep.tile([P, L], F32, name="root")
         nc.scalar.activation(out=root[:], in_=tot[:], func=ACT.Sqrt)
         res = keep.tile([P, L], F32, name="res")

@@ -21,9 +21,10 @@ DO = 2048
 G1 = 8
 G2 = 4
 NCG = 4
-NC = 16
-VC = 2
-LAG = 1
+VPER = 5
+NV = 25
+LAG = 3
+KEEP_EVERY = 4
 
 FLOPS = 2 * B * (2 * DH) * DO + 2 * B * DO * DO
 
@@ -35,11 +36,12 @@ def tile_relationembedding_w_kernel(
     with ExitStack() as ctx:
         ctx.enter_context(tc.manual_schedule())
         keep = ctx.enter_context(tc.tile_pool(name="keep", bufs=1))
-        rpool = ctx.enter_context(tc.tile_pool(name="rpool", bufs=4))
+        rpool = ctx.enter_context(tc.tile_pool(name="rpool", bufs=6))
+        jpool = ctx.enter_context(tc.tile_pool(name="jpool", bufs=2))
         psum = ctx.enter_context(tc.psum_pool(name="psum", bufs=8))
 
         def bank(name, shape=(P, 512), dtype=F32):
-            return psum.tile(list(shape), dtype, name=name, tag="bank")
+            return psum.tile(list(shape), dtype, name=name, tag="bank", bufs=7)
 
         ident_f = keep.tile([P, P], F32, name="ident_f")
         ident_b = keep.tile([P, P], BF16, name="ident_b")
@@ -53,6 +55,8 @@ def tile_relationembedding_w_kernel(
         nc.vector.memset(zt[:], 0.0)
         one = keep.tile([P, 1], F32, name="one")
         nc.vector.memset(one[:], 1.0)
+        acc_s = keep.tile([P, NCG, L], F32, name="acc_s")
+        nc.vector.memset(acc_s[:], 0.0)
         one2 = keep.tile([P, 1], F32, name="one2")
         nc.scalar.activation(out=one2[:], in_=one[:], func=ACT.Sqrt)
 
@@ -197,54 +201,66 @@ def tile_relationembedding_w_kernel(
                     scale=1.0,
                 )
 
-        for cg in range(NCG):
-            layer2(cg)
-
-        tot = keep.tile([P, L], F32, name="tot")
+        stats = keep.tile([P, NCG, NV, 6], F32, name="stats")
         pending = []
 
-        def reduce_bank(k, tp):
-            nc.vector.tensor_reduce(
-                out=tot[:, 4 * k : 4 * k + 4],
-                in_=tp[:].rearrange("p (l d) -> p l d", d=P),
-                axis=AX.X,
-                op=ALU.add,
-            )
-
-        mid = (VC + NC) // 2
-        tp = None
-        for l in range(L):
-            r = rpool.tile([P, NC, B], F32, name="r", tag="r")
-            for c in range(NC):
-                nc.vector.tensor_scalar(
-                    out=r[:, c, :],
-                    in0=emb[c // 4][:, c % 4, :],
-                    scalar1=lab_t[:, c, l : l + 1],
-                    scalar2=0.0,
-                    op0=ALU.subtract,
-                    op1=ALU.min,
+        def sum_squares(cg, l, tp):
+            if l % VPER == VPER - 1:
+                nc.vector.bn_stats(out=stats[:, cg, l // VPER, :], in_=tp[:])
+            else:
+                junk = jpool.tile([P, 512], F32, name="junk", tag="junk")
+                nc.scalar.activation(
+                    out=junk[:], in_=tp[:], func=ACT.Square, accum_out=acc_s[:, cg, l : l + 1]
                 )
-            nc.vector.tensor_tensor(out=r[:, 0:VC, :], in0=r[:, 0:VC, :], in1=r[:, 0:VC, :], op=ALU.mult)
-            nc.scalar.activation(out=r[:, VC:mid, :], in_=r[:, VC:mid, :], func=ACT.Square)
-            nc.scalar.activation(out=r[:, mid:NC, :], in_=r[:, mid:NC, :], func=ACT.Square)
-            if l % 4 == 0:
+
+        layer2(0)
+        scrap = psum.tile([P, 512], F32, name="scrap", tag="scrap", bufs=1)
+        for cg in range(NCG):
+            for l in range(L):
+                if l % KEEP_EVERY == 0:
+                    nc.tensor.matmul_mx(
+                        out=scrap[:],
+                        lhsT=hq[:, 0, :].bitcast(FP8X4),
+                        lhsT_scale=hs[:, 0, :],
+                        rhs=w1[0][:, 0:512].bitcast(FP8X4),
+                        rhs_scale=planes[0][0:P, 0:512],
+                        start=True,
+                        stop=True,
+                    )
+                r = rpool.tile([P, 4, B], F32, name="r", tag="r")
+                for j in range(4):
+                    nc.vector.tensor_scalar(
+                        out=r[:, j, :],
+                        in0=emb[cg][:, j, :],
+                        scalar1=lab_t[:, 4 * cg + j, l : l + 1],
+                        scalar2=0.0,
+                        op0=ALU.subtract,
+                        op1=ALU.min,
+                    )
                 tp = bank("tp")
-            for c in range(NC):
-                nc.tensor.matmul(
-                    out=tp[:, P * (l % 4) : P * (l % 4 + 1)],
-                    lhsT=r[:, c, :],
-                    rhs=ident_f[:],
-                    is_transpose=True,
-                    start=(c == 0),
-                    stop=(c == NC - 1),
-                )
-            if l % 4 == 3:
-                pending.append((l // 4, tp))
+                for j in range(4):
+                    nc.tensor.transpose(tp[:, P * j : P * (j + 1)], r[:, j, :], ident_f[:])
+                pending.append((cg, l, tp))
                 if len(pending) > LAG:
-                    reduce_bank(*pending.pop(0))
+                    sum_squares(*pending.pop(0))
+                if l == 64 and cg + 1 < NCG:
+                    layer2(cg + 1)
         for item in pending:
-            reduce_bank(*item)
+            sum_squares(*item)
 
+        tot = keep.tile([P, L], F32, name="tot")
+        nc.vector.tensor_reduce(out=tot[:], in_=acc_s[:].rearrange("p c l -> p l c"), axis=AX.X, op=ALU.add)
+        st = stats[:].rearrange("p c v (e s) -> p c v e s", s=3)
+        msq = keep.tile([P, NCG, NV, 2], F32, name="msq")
+        nc.vector.tensor_tensor(out=msq[:], in0=st[:, :, :, :, 1], in1=st[:, :, :, :, 1], op=ALU.mult)
+        ssq = keep.tile([P, NCG, NV, 2], F32, name="ssq")
+        nc.vector.scalar_tensor_tensor(
+            out=ssq[:], in0=msq[:], scalar=256.0, in1=st[:, :, :, :, 2], op0=ALU.mult, op1=ALU.add
+        )
+        sum_v = keep.tile([P, NV], F32, name="sum_v")
+        nc.vector.tensor_reduce(out=sum_v[:], in_=ssq[:].rearrange("p c v e -> p v c e"), axis=AX.XY, op=ALU.add)
+        tot_v = tot[:, 0 : VPER * NV].rearrange("p (v f) -> p v f", f=VPER)[:, :, VPER - 1]
+        nc.vector.tensor_tensor(out=tot_v, in0=tot_v, in1=sum_v[:], op=ALU.add)
         root = keep.tile([P, L], F32, name="root")
         nc.scalar.activation(out=root[:], in_=tot[:], func=ACT.Sqrt)
         res = keep.tile([P, L], F32, name="res")

@@ -217,7 +217,8 @@ def tile_relationembedding_w_kernel(
         scrap = psum.tile([P, 512], F32, name="scrap", tag="scrap", bufs=1)
         for cg in range(NCG):
             for l in range(L):
-                if l % KEEP_EVERY == 0:
+                plain_first = l % (2 * KEEP_EVERY) == KEEP_EVERY
+                if l % (2 * KEEP_EVERY) == 0:
                     nc.tensor.matmul_mx(
                         out=scrap[:],
                         lhsT=hq[:, 0, :].bitcast(FP8X4),
@@ -239,7 +240,10 @@ def tile_relationembedding_w_kernel(
                     )
                 tp = bank("tp")
                 for j in range(4):
-                    nc.tensor.transpose(tp[:, P * j : P * (j + 1)], r[:, j, :], ident_f[:])
+                    if plain_first and j == 0:
+                        nc.tensor.matmul(out=tp[:, 0:P], lhsT=r[:, 0, :], rhs=ident_f[:], start=True, stop=True)
+                    else:
+                        nc.tensor.transpose(tp[:, P * j : P * (j + 1)], r[:, j, :], ident_f[:])
                 pending.append((cg, l, tp))
                 if len(pending) > LAG:
                     sum_squares(*pending.pop(0))

@@ -21,8 +21,10 @@ DO = 2048
 G1 = 8
 G2 = 4
 NCG = 4
-VPER = 5
-NV = 25
+V_MOD = 9
+V_RES = (4, 8)
+NVB = L // V_MOD
+NV = NVB * len(V_RES)
 LAG = 3
 KEEP_EVERY = 4
 
@@ -205,8 +207,9 @@ def tile_relationembedding_w_kernel(
         pending = []
 
         def sum_squares(cg, l, tp):
-            if l % VPER == VPER - 1:
-                nc.vector.bn_stats(out=stats[:, cg, l // VPER, :], in_=tp[:])
+            if l % V_MOD in V_RES and l // V_MOD < NVB:
+                v = len(V_RES) * (l // V_MOD) + V_RES.index(l % V_MOD)
+                nc.vector.bn_stats(out=stats[:, cg, v, :], in_=tp[:])
             else:
                 junk = jpool.tile([P, 512], F32, name="junk", tag="junk")
                 nc.scalar.activation(
@@ -263,8 +266,10 @@ def tile_relationembedding_w_kernel(
         )
         sum_v = keep.tile([P, NV], F32, name="sum_v")
         nc.vector.tensor_reduce(out=sum_v[:], in_=ssq[:].rearrange("p c v e -> p v c e"), axis=AX.XY, op=ALU.add)
-        tot_v = tot[:, 0 : VPER * NV].rearrange("p (v f) -> p v f", f=VPER)[:, :, VPER - 1]
-        nc.vector.tensor_tensor(out=tot_v, in0=tot_v, in1=sum_v[:], op=ALU.add)
+        tot_v = tot[:, 0 : V_MOD * NVB].rearrange("p (v f) -> p v f", f=V_MOD)[:, :, V_RES[0] : V_MOD : V_RES[1] - V_RES[0]]
+        nc.vector.tensor_tensor(
+            out=tot_v, in0=tot_v, in1=sum_v[:].rearrange("p (v k) -> p v k", k=len(V_RES)), op=ALU.add
+        )
         root = keep.tile([P, L], F32, name="root")
         nc.scalar.activation(out=root[:], in_=tot[:], func=ACT.Sqrt)
         res = keep.tile([P, L], F32, name="res")

@@ -25,7 +25,7 @@ V_MOD = 9
 V_RES = (4, 8)
 NVB = L // V_MOD
 NV = NVB * len(V_RES)
-LAG = 3
+LAG = 6
 KEEP_EVERY = 4
 
 FLOPS = 2 * B * (2 * DH) * DO + 2 * B * DO * DO

@@ -50,11 +50,11 @@ def tile_relationembedding_w_kernel(
         make_identity(nc, ident_f[:])
         make_identity(nc, ident_b[:])
 
+        zt = keep.tile([P, P], BF16, name="zt")
+        nc.vector.memset(zt[:], 0.0)
         planes = [keep.tile([P, 2048], U8, name="planes%d" % i, align_bytes=64) for i in range(3)]
         for pl in planes:
             nc.vector.memset(pl[:].bitcast(I32), 0)
-        zt = keep.tile([P, P], BF16, name="zt")
-        nc.vector.memset(zt[:], 0.0)
         one = keep.tile([P, 1], F32, name="one")
         nc.vector.memset(one[:], 1.0)
         acc_s = keep.tile([P, NCG, L], F32, name="acc_s")
@@ -62,20 +62,17 @@ def tile_relationembedding_w_kernel(
         one2 = keep.tile([P, 1], F32, name="one2")
         nc.scalar.activation(out=one2[:], in_=one[:], func=ACT.Sqrt)
 
-        x_sb = keep.tile([P, 2 * DH], BF16, name="x_sb")
-        nc.sync.dma_start(out=x_sb[:, 0:DH], in_=sbj_vec[:, :])
-        nc.sync.dma_start(out=x_sb[:, DH : 2 * DH], in_=obj_vec[:, :])
-        lab_sb = keep.tile([P, DO], BF16, name="lab_sb")
-        nc.sync.dma_start(out=lab_sb[:], in_=label_vecs[:, :])
         nc.sync.dma_start(out=zt[0:16, :], in_=b2.rearrange("(c p) -> c p", p=P))
-        b1b = keep.tile([P, DO], BF16, name="b1b")
-        nc.sync.dma_start(out=b1b[:], in_=b1.partition_broadcast(P))
+        nc.sync.dma_start(out=zt[16:32, :], in_=b1.rearrange("(c p) -> c p", p=P))
         for i, src in ((0, W1_scales[0:4]), (1, W1_scales[4:8]), (2, W2_scales)):
             for q in range(4):
                 nc.sync.dma_start(
                     out=planes[i][32 * q : 32 * q + 16, :].bitcast(I32),
                     in_=src[:, 4 * q : 4 * q + 4, :].bitcast(I32),
                 )
+        x_sb = keep.tile([P, 2 * DH], BF16, name="x_sb")
+        nc.sync.dma_start(out=x_sb[:, 0:DH], in_=sbj_vec[:, :])
+        nc.sync.dma_start(out=x_sb[:, DH : 2 * DH], in_=obj_vec[:, :])
         w1 = []
         for g in range(G1):
             w = keep.tile([P, DO], U32, name="w1_%d" % g, align_bytes=64)
@@ -91,6 +88,25 @@ def tile_relationembedding_w_kernel(
                 out=w[:].bitcast(I32), in_=w2_view[:, :, 2048 * cg : 2048 * (cg + 1)].bitcast(I32)
             )
             w2.append(w)
+            if cg == 0:
+                lab_sb = keep.tile([P, DO], BF16, name="lab_sb")
+                nc.sync.dma_start(out=lab_sb[:], in_=label_vecs[:, :])
+
+        bp = bank("bp", (P, 1024), BF16)
+        nc.tensor.transpose(bp[:, 0:P], zt[:], ident_b[:])
+        b2_t = keep.tile([P, 16], F32, name="b2_t")
+        nc.vector.tensor_copy(out=b2_t[:], in_=bp[:, 0:16])
+        b1_t = keep.tile([P, 16], BF16, name="b1_t")
+        nc.vector.tensor_copy(out=b1_t[:], in_=bp[:, 16:32])
+        b1b = keep.tile([P, DO], BF16, name="b1b")
+
+        def spread_b1():
+            for i in range(2):
+                bb = bank("bb%d" % i, (P, 8, P), BF16)
+                for cc in range(8):
+                    c = 8 * i + cc
+                    nc.tensor.transpose(bb[:, cc, :], b1_t[:, c : c + 1].to_broadcast([P, P]), ident_b[:])
+                nc.scalar.copy(out=b1b[:, 1024 * i : 1024 * (i + 1)], in_=bb[:].rearrange("p c n -> p (c n)"))
 
         gx = keep.tile([P, G1, B, 4], BF16, name="gx", align_bytes=64)
         xq = keep.tile([P, G1, B], U32, name="xq", align_bytes=64)
@@ -115,20 +131,7 @@ def tile_relationembedding_w_kernel(
             else:
                 nc.scalar.copy(out=gx_words[:, 2 * i : 2 * i + 2], in_=src)
 
-        lab_t = keep.tile([P, 16, L], F32, name="lab_t")
-        for i in range(2):
-            lp = bank("lp%d" % i, (P, 8, L), BF16)
-            for cc in range(8):
-                c = 8 * i + cc
-                nc.tensor.transpose(lp[:, cc, :], lab_sb[:, P * c : P * (c + 1)], ident_b[:])
-            if i == 0:
-                nc.scalar.copy(out=lab_t[:, 0:8, :], in_=lp[:])
-            else:
-                nc.vector.tensor_copy(out=lab_t[:, 8:16, :], in_=lp[:])
-        bp = bank("bp", (P, 1024), BF16)
-        nc.tensor.transpose(bp[:, 0:P], zt[:], ident_b[:])
-        b2_t = keep.tile([P, 16], F32, name="b2_t")
-        nc.vector.tensor_copy(out=b2_t[:], in_=bp[:, 0:16])
+        spread_b1()
 
         for h in range(2):
             nc.vector.quantize_mx(
@@ -176,6 +179,17 @@ def tile_relationembedding_w_kernel(
             scales=hs[:].rearrange("p g b -> p (g b)"),
             in_=gh[:].rearrange("p g b t -> p (g b t)"),
         )
+
+        lab_t = keep.tile([P, 16, L], F32, name="lab_t")
+        for i in range(2):
+            lp = bank("lp%d" % i, (P, 8, L), BF16)
+            for cc in range(8):
+                c = 8 * i + cc
+                nc.tensor.transpose(lp[:, cc, :], lab_sb[:, P * c : P * (c + 1)], ident_b[:])
+            if i == 0:
+                nc.scalar.copy(out=lab_t[:, 0:8, :], in_=lp[:])
+            else:
+                nc.vector.tensor_copy(out=lab_t[:, 8:16, :], in_=lp[:])
 
         emb = [keep.tile([P, 4, B], F32, name="emb%d" % cg) for cg in range(NCG)]
 

@@ -26,7 +26,7 @@ V_RES = (4, 8)
 NVB = L // V_MOD
 NV = NVB * len(V_RES)
 LAG = 6
-KEEP_EVERY = 4
+KEEP_EVERY = 14
 
 FLOPS = 2 * B * (2 * DH) * DO + 2 * B * DO * DO
 
@@ -234,17 +234,6 @@ def tile_relationembedding_w_kernel(
         scrap = psum.tile([P, 512], F32, name="scrap", tag="scrap", bufs=1)
         for cg in range(NCG):
             for l in range(L):
-                plain_first = l % (2 * KEEP_EVERY) == KEEP_EVERY
-                if l % (2 * KEEP_EVERY) == 0:
-                    nc.tensor.matmul_mx(
-                        out=scrap[:],
-                        lhsT=hq[:, 0, :].bitcast(FP8X4),
-                        lhsT_scale=hs[:, 0, :],
-                        rhs=w1[0][:, 0:512].bitcast(FP8X4),
-                        rhs_scale=planes[0][0:P, 0:512],
-                        start=True,
-                        stop=True,
-                    )
                 r = rpool.tile([P, 4, B], F32, name="r", tag="r")
                 for j in range(4):
                     nc.vector.tensor_scalar(
@@ -257,10 +246,17 @@ def tile_relationembedding_w_kernel(
                     )
                 tp = bank("tp")
                 for j in range(4):
-                    if plain_first and j == 0:
-                        nc.tensor.matmul(out=tp[:, 0:P], lhsT=r[:, 0, :], rhs=ident_f[:], start=True, stop=True)
-                    else:
-                        nc.tensor.transpose(tp[:, P * j : P * (j + 1)], r[:, j, :], ident_f[:])
+                    if (4 * (L * cg + l) + j) % KEEP_EVERY == 0:
+                        nc.tensor.matmul_mx(
+                            out=scrap[:],
+                            lhsT=hq[:, 0, :].bitcast(FP8X4),
+                            lhsT_scale=hs[:, 0, :],
+                            rhs=w1[0][:, 0:512].bitcast(FP8X4),
+                            rhs_scale=planes[0][0:P, 0:512],
+                            start=True,
+                            stop=True,
+                        )
+                    nc.tensor.transpose(tp[:, P * j : P * (j + 1)], r[:, j, :], ident_f[:])
                 pending.append((cg, l, tp))
                 if len(pending) > LAG:
                     sum_squares(*pending.pop(0))

@@ -76,10 +76,17 @@ def tile_relationembedding_w_kernel(
         w1 = []
         for g in range(G1):
             w = keep.tile([P, DO], U32, name="w1_%d" % g, align_bytes=64)
-            nc.sync.dma_start(
-                out=w[:].bitcast(I32), in_=W1_words[g].rearrange("p n t -> p (n t)").bitcast(I32)
-            )
+            w_hbm = W1_words[g].rearrange("p n t -> p (n t)")
+            pieces = 4 if g == G1 - 1 else 1
+            wide = DO // pieces
+            for i in range(pieces):
+                nc.sync.dma_start(
+                    out=w[:, wide * i : wide * (i + 1)].bitcast(I32),
+                    in_=w_hbm[:, 4 * wide * i : 4 * wide * (i + 1)].bitcast(I32),
+                )
             w1.append(w)
+        lab_sb = keep.tile([P, DO], BF16, name="lab_sb")
+        nc.sync.dma_start(out=lab_sb[:, 0:512], in_=label_vecs[:, 0:512])
         w2 = []
         w2_view = W2_words.rearrange("g p n t -> p g (n t)")
         for cg in range(NCG):
@@ -89,8 +96,7 @@ def tile_relationembedding_w_kernel(
             )
             w2.append(w)
             if cg == 0:
-                lab_sb = keep.tile([P, DO], BF16, name="lab_sb")
-                nc.sync.dma_start(out=lab_sb[:], in_=label_vecs[:, :])
+                nc.sync.dma_start(out=lab_sb[:, 512:DO], in_=label_vecs[:, 512:DO])
 
         bp = bank("bp", (P, 1024), BF16)
         nc.tensor.transpose(bp[:, 0:P], zt[:], ident_b[:])
@@ -165,6 +171,12 @@ def tile_relationembedding_w_kernel(
             cols = slice(512 * g, 512 * (g + 1))
             nc.vector.tensor_tensor(out=h32[:, cols], in0=acc[g][:], in1=b1b[:, cols], op=ALU.add)
             nc.scalar.activation(out=hb[:, cols], in_=h32[:, cols], func=ACT.Relu)
+
+        def quantize_hidden(g):
+            nc.vector.quantize_mx(
+                out=hq[:, g, :].bitcast(FP8X4), scales=hs[:, g, :], in_=gh[:, g].rearrange("p b t -> p (b t)")
+            )
+
         for g in range(G2):
             ht = bank("ht%d" % g, (P, 8, B), BF16)
             for t in range(4):
@@ -174,47 +186,49 @@ def tile_relationembedding_w_kernel(
                 nc.vector.tensor_copy(out=gh[:, g], in_=src)
             else:
                 nc.scalar.copy(out=gh[:, g], in_=src)
-        nc.vector.quantize_mx(
-            out=hq[:].rearrange("p g b -> p (g b)").bitcast(FP8X4),
-            scales=hs[:].rearrange("p g b -> p (g b)"),
-            in_=gh[:].rearrange("p g b t -> p (g b t)"),
-        )
+            if g == 0:
+                quantize_hidden(0)
+            elif g == 2:
+                quantize_hidden(1)
+                quantize_hidden(2)
+            elif g == 3:
+                quantize_hidden(3)
 
         lab_t = keep.tile([P, 16, L], F32, name="lab_t")
-        for i in range(2):
-            lp = bank("lp%d" % i, (P, 8, L), BF16)
-            for cc in range(8):
-                c = 8 * i + cc
-                nc.tensor.transpose(lp[:, cc, :], lab_sb[:, P * c : P * (c + 1)], ident_b[:])
-            if i == 0:
-                nc.scalar.copy(out=lab_t[:, 0:8, :], in_=lp[:])
-            else:
-                nc.vector.tensor_copy(out=lab_t[:, 8:16, :], in_=lp[:])
+
+        def turn_labels(c0, c1, engine_copy):
+            lp = bank("lp%d" % c0, (P, 8, L), BF16)
+            for c in range(c0, c1):
+                nc.tensor.transpose(lp[:, c - c0, :], lab_sb[:, P * c : P * (c + 1)], ident_b[:])
+            engine_copy(out=lab_t[:, c0:c1, :], in_=lp[:, 0 : c1 - c0, :])
+
+        turn_labels(0, 4, nc.vector.tensor_copy)
 
         emb = [keep.tile([P, 4, B], F32, name="emb%d" % cg) for cg in range(NCG)]
 
-        def layer2(cg):
-            ep = bank("ep%d" % cg)
-            for j in range(4):
+        def layer2(cg, own_banks):
+            if own_banks:
+                eps = [bank("ep%d_%d" % (cg, j))[:, 0:P] for j in range(4)]
+                order = [(j, g) for g in range(G2) for j in range(4)]
+            else:
+                ep = bank("ep%d" % cg)
+                eps = [ep[:, P * j : P * (j + 1)] for j in range(4)]
+                order = [(j, g) for j in range(4) for g in range(G2)]
+            for j, g in order:
                 cols = slice(P * j, P * (j + 1))
-                for g in range(G2):
-                    nc.tensor.matmul_mx(
-                        out=ep[:, cols],
-                        lhsT=w2[cg][:, g, cols].bitcast(FP8X4),
-                        lhsT_scale=planes[2][4 * g : P, 512 * cg + P * j : 512 * cg + P * (j + 1)],
-                        rhs=hq[:, g, :].bitcast(FP8X4),
-                        rhs_scale=hs[:, g, :],
-                        start=(g == 0),
-                        stop=(g == G2 - 1),
-                    )
+                nc.tensor.matmul_mx(
+                    out=eps[j],
+                    lhsT=w2[cg][:, g, cols].bitcast(FP8X4),
+                    lhsT_scale=planes[2][4 * g : P, 512 * cg + P * j : 512 * cg + P * (j + 1)],
+                    rhs=hq[:, g, :].bitcast(FP8X4),
+                    rhs_scale=hs[:, g, :],
+                    start=(g == 0),
+                    stop=(g == G2 - 1),
+                )
             for j in range(4):
                 c = 4 * cg + j
                 nc.scalar.activation(
-                    out=emb[cg][:, j, :],
-                    in_=ep[:, P * j : P * (j + 1)],
-                    func=ACT.Identity,
-                    bias=b2_t[:, c : c + 1],
-                    scale=1.0,
+                    out=emb[cg][:, j, :], in_=eps[j], func=ACT.Identity, bias=b2_t[:, c : c + 1], scale=1.0
                 )
 
         stats = keep.tile([P, NCG, NV, 6], F32, name="stats")
@@ -230,7 +244,9 @@ def tile_relationembedding_w_kernel(
                     out=junk[:], in_=tp[:], func=ACT.Square, accum_out=acc_s[:, cg, l : l + 1]
                 )
 
-        layer2(0)
+        layer2(0, True)
+        turn_labels(4, 12, nc.scalar.copy)
+        turn_labels(12, 16, nc.scalar.copy)
         scrap = psum.tile([P, 512], F32, name="scrap", tag="scrap", bufs=1)
         for cg in range(NCG):
             for l in range(L):
@@ -261,7 +277,7 @@ def tile_relationembedding_w_kernel(
                 if len(pending) > LAG:
                     sum_squares(*pending.pop(0))
                 if l == 64 and cg + 1 < NCG:
-                    layer2(cg + 1)
+                    layer2(cg + 1, False)
         for item in pending:
             sum_squares(*item)
 

@@ -25,8 +25,8 @@ V_MOD = 9
 V_RES = (4, 8)
 NVB = L // V_MOD
 NV = NVB * len(V_RES)
-LAG = 6
-KEEP_EVERY = 14
+LAG = 5
+KEEP_EVERY = 4
 
 FLOPS = 2 * B * (2 * DH) * DO + 2 * B * DO * DO
 
@@ -43,7 +43,7 @@ def tile_relationembedding_w_kernel(
         psum = ctx.enter_context(tc.psum_pool(name="psum", bufs=8))
 
         def bank(name, shape=(P, 512), dtype=F32):
-            return psum.tile(list(shape), dtype, name=name, tag="bank", bufs=7)
+            return psum.tile(list(shape), dtype, name=name, tag="bank", bufs=8)
 
         ident_f = keep.tile([P, P], F32, name="ident_f")
         ident_b = keep.tile([P, P], BF16, name="ident_b")
@@ -194,15 +194,16 @@ def tile_relationembedding_w_kernel(
             elif g == 3:
                 quantize_hidden(3)
 
-        lab_t = keep.tile([P, 16, L], F32, name="lab_t")
+        def turn_labels(cg):
+            lp = bank("lab%d" % cg, (P, 4, L))
+            for j in range(4):
+                c = 4 * cg + j
+                nc.tensor.matmul(
+                    out=lp[:, j, :], lhsT=lab_sb[:, P * c : P * (c + 1)], rhs=ident_b[:], start=True, stop=True
+                )
+            return lp
 
-        def turn_labels(c0, c1, engine_copy):
-            lp = bank("lp%d" % c0, (P, 8, L), BF16)
-            for c in range(c0, c1):
-                nc.tensor.transpose(lp[:, c - c0, :], lab_sb[:, P * c : P * (c + 1)], ident_b[:])
-            engine_copy(out=lab_t[:, c0:c1, :], in_=lp[:, 0 : c1 - c0, :])
-
-        turn_labels(0, 4, nc.vector.tensor_copy)
+        lab_next = turn_labels(0)
 
         emb = [keep.tile([P, 4, B], F32, name="emb%d" % cg) for cg in range(NCG)]
 
@@ -245,39 +246,39 @@ def tile_relationembedding_w_kernel(
                 )
 
         layer2(0, True)
-        turn_labels(4, 12, nc.scalar.copy)
-        turn_labels(12, 16, nc.scalar.copy)
-        scrap = psum.tile([P, 512], F32, name="scrap", tag="scrap", bufs=1)
         for cg in range(NCG):
+            lab_t = lab_next
             for l in range(L):
                 r = rpool.tile([P, 4, B], F32, name="r", tag="r")
                 for j in range(4):
                     nc.vector.tensor_scalar(
                         out=r[:, j, :],
                         in0=emb[cg][:, j, :],
-                        scalar1=lab_t[:, 4 * cg + j, l : l + 1],
+                        scalar1=lab_t[:, j, l : l + 1],
                         scalar2=0.0,
                         op0=ALU.subtract,
                         op1=ALU.min,
                     )
                 tp = bank("tp")
+                if l % KEEP_EVERY == 0:
+                    nc.tensor.matmul_mx(
+                        out=tp[:],
+                        lhsT=hq[:, 0, :].bitcast(FP8X4),
+                        lhsT_scale=hs[:, 0, :],
+                        rhs=w1[0][:, 0:512].bitcast(FP8X4),
+                        rhs_scale=planes[0][0:P, 0:512],
+                        start=True,
+                        stop=True,
+                    )
                 for j in range(4):
-                    if (4 * (L * cg + l) + j) % KEEP_EVERY == 0:
-                        nc.tensor.matmul_mx(
-                            out=scrap[:],
-                            lhsT=hq[:, 0, :].bitcast(FP8X4),
-                            lhsT_scale=hs[:, 0, :],
-                            rhs=w1[0][:, 0:512].bitcast(FP8X4),
-                            rhs_scale=planes[0][0:P, 0:512],
-                            start=True,
-                            stop=True,
-                        )
                     nc.tensor.transpose(tp[:, P * j : P * (j + 1)], r[:, j, :], ident_f[:])
                 pending.append((cg, l, tp))
                 if len(pending) > LAG:
                     sum_squares(*pending.pop(0))
                 if l == 64 and cg + 1 < NCG:
                     layer2(cg + 1, False)
+                if l == 96 and cg + 1 < NCG:
+                    lab_next = turn_labels(cg + 1)
         for item in pending:
             sum_squares(*item)
 

@@ -245,6 +245,35 @@ def tile_relationembedding_w_kernel(
                     out=junk[:], in_=tp[:], func=ACT.Square, accum_out=acc_s[:, cg, l : l + 1]
                 )
 
+        tot = keep.tile([P, L], F32, name="tot")
+        tot_v = tot[:, 0 : V_MOD * NVB].rearrange("p (v f) -> p v f", f=V_MOD)[:, :, V_RES[0] : V_MOD : V_RES[1] - V_RES[0]]
+
+        def vector_sum_steps(c0, c1):
+            st = stats[:, c0:c1].rearrange("p c v (e s) -> p c v e s", s=3)
+            msq = keep.tile([P, c1 - c0, NV, 2], F32, name="msq%d" % c0)
+            ssq = keep.tile([P, c1 - c0, NV, 2], F32, name="ssq%d" % c0)
+            sum_v = keep.tile([P, NV], F32, name="sum_v%d" % c0)
+            return [
+                lambda: nc.vector.tensor_tensor(
+                    out=msq[:], in0=st[:, :, :, :, 1], in1=st[:, :, :, :, 1], op=ALU.mult
+                ),
+                lambda: nc.vector.scalar_tensor_tensor(
+                    out=ssq[:], in0=msq[:], scalar=256.0, in1=st[:, :, :, :, 2], op0=ALU.mult, op1=ALU.add
+                ),
+                lambda: nc.vector.tensor_reduce(
+                    out=sum_v[:], in_=ssq[:].rearrange("p c v e -> p v c e"), axis=AX.XY, op=ALU.add
+                ),
+                lambda: nc.vector.tensor_tensor(
+                    out=tot_v, in0=tot_v, in1=sum_v[:].rearrange("p (v k) -> p v k", k=len(V_RES)), op=ALU.add
+                ),
+            ]
+
+        early = [
+            lambda: nc.vector.tensor_reduce(
+                out=tot[:], in_=acc_s[:, 0 : NCG - 1, :].rearrange("p c l -> p l c"), axis=AX.X, op=ALU.add
+            )
+        ] + vector_sum_steps(0, NCG - 1)
+
         layer2(0, True)
         for cg in range(NCG):
             lab_t = lab_next
@@ -279,26 +308,16 @@ def tile_relationembedding_w_kernel(
                     layer2(cg + 1, False)
                 if l == 96 and cg + 1 < NCG:
                     lab_next = turn_labels(cg + 1)
+                if cg == NCG - 1 and l >= 4 * LAG and early:
+                    early.pop(0)()
         for item in pending:
             sum_squares(*item)
 
-        tot = keep.tile([P, L], F32, name="tot")
-        nc.vector.tensor_reduce(out=tot[:], in_=acc_s[:].rearrange("p c l -> p l c"), axis=AX.X, op=ALU.add)
-        st = stats[:].rearrange("p c v (e s) -> p c v e s", s=3)
-        msq = keep.tile([P, NCG, NV, 2], F32, name="msq")
-        nc.vector.tensor_tensor(out=msq[:], in0=st[:, :, :, :, 1], in1=st[:, :, :, :, 1], op=ALU.mult)
-        ssq = keep.tile([P, NCG, NV, 2], F32, name="ssq")
-        nc.vector.scalar_tensor_tensor(
-            out=ssq[:], in0=msq[:], scalar=256.0, in1=st[:, :, :, :, 2], op0=ALU.mult, op1=ALU.add
-        )
-        sum_v = keep.tile([P, NV], F32, name="sum_v")
-        nc.vector.tensor_reduce(out=sum_v[:], in_=ssq[:].rearrange("p c v e -> p v c e"), axis=AX.XY, op=ALU.add)
-        tot_v = tot[:, 0 : V_MOD * NVB].rearrange("p (v f) -> p v f", f=V_MOD)[:, :, V_RES[0] : V_MOD : V_RES[1] - V_RES[0]]
-        nc.vector.tensor_tensor(
-            out=tot_v, in0=tot_v, in1=sum_v[:].rearrange("p (v k) -> p v k", k=len(V_RES)), op=ALU.add
-        )
+        for step in vector_sum_steps(NCG - 1, NCG):
+            step()
+        nc.vector.tensor_tensor(out=tot[:], in0=tot[:], in1=acc_s[:, NCG - 1, :], op=ALU.add)
         root = keep.tile([P, L], F32, name="root")
         nc.scalar.activation(out=root[:], in_=tot[:], func=ACT.Sqrt)
         res = keep.tile([P, L], F32, name="res")
-        nc.vector.tensor_scalar_mul(out=res[:], in0=root[:], scalar1=-1.0)
+        nc.scalar.mul(out=res[:], in_=root[:], mul=-1.0)
         nc.sync.dma_start(out=out[:, :], in_=res[:])

from contextlib import ExitStack

import concourse.mybir as mybir
from concourse.masks import make_identity

F32 = mybir.dt.float32
BF16 = mybir.dt.bfloat16
I32 = mybir.dt.int32
U32 = mybir.dt.uint32
U8 = mybir.dt.uint8
FP8X4 = mybir.dt.float8_e4m3fn_x4
ALU = mybir.AluOpType
ACT = mybir.ActivationFunctionType
AX = mybir.AxisListType

P = 128
B = 128
L = 128
DH = 2048
DO = 2048
G1 = 8
G2 = 4
NCG = 4
V_MOD = 9
V_RES = (4, 8)
NVB = L // V_MOD
NV = NVB * len(V_RES)
LAG = 5
KEEP_EVERY = 4

FLOPS = 2 * B * (2 * DH) * DO + 2 * B * DO * DO


def tile_relationembedding_w_kernel(
    tc, sbj_vec, obj_vec, W1_words, W1_scales, b1, W2_words, W2_scales, b2, label_vecs, out
):
    nc = tc.nc
    with ExitStack() as ctx:
        ctx.enter_context(tc.manual_schedule())
        keep = ctx.enter_context(tc.tile_pool(name="keep", bufs=1))
        rpool = ctx.enter_context(tc.tile_pool(name="rpool", bufs=6))
        jpool = ctx.enter_context(tc.tile_pool(name="jpool", bufs=2))
        psum = ctx.enter_context(tc.psum_pool(name="psum", bufs=8))

        def bank(name, shape=(P, 512), dtype=F32):
            return psum.tile(list(shape), dtype, name=name, tag="bank", bufs=8)

        ident_f = keep.tile([P, P], F32, name="ident_f")
        ident_b = keep.tile([P, P], BF16, name="ident_b")
        make_identity(nc, ident_f[:])
        make_identity(nc, ident_b[:])

        zt = keep.tile([P, P], BF16, name="zt")
        nc.vector.memset(zt[:], 0.0)
        planes = [keep.tile([P, 2048], U8, name="planes%d" % i, align_bytes=64) for i in range(3)]
        for pl in planes:
            nc.vector.memset(pl[:].bitcast(I32), 0)
        one = keep.tile([P, 1], F32, name="one")
        nc.vector.memset(one[:], 1.0)
        acc_s = keep.tile([P, NCG, L], F32, name="acc_s")
        nc.vector.memset(acc_s[:], 0.0)
        one2 = keep.tile([P, 1], F32, name="one2")
        nc.scalar.activation(out=one2[:], in_=one[:], func=ACT.Sqrt)

        nc.sync.dma_start(out=zt[0:16, :], in_=b2.rearrange("(c p) -> c p", p=P))
        nc.sync.dma_start(out=zt[16:32, :], in_=b1.rearrange("(c p) -> c p", p=P))
        for i, src in ((0, W1_scales[0:4]), (1, W1_scales[4:8]), (2, W2_scales)):
            for q in range(4):
                nc.sync.dma_start(
                    out=planes[i][32 * q : 32 * q + 16, :].bitcast(I32),
                    in_=src[:, 4 * q : 4 * q + 4, :].bitcast(I32),
                )
        x_sb = keep.tile([P, 2 * DH], BF16, name="x_sb")
        nc.sync.dma_start(out=x_sb[:, 0:DH], in_=sbj_vec[:, :])
        nc.sync.dma_start(out=x_sb[:, DH : 2 * DH], in_=obj_vec[:, :])
        w1 = []
        for g in range(G1):
            w = keep.tile([P, DO], U32, name="w1_%d" % g, align_bytes=64)
            w_hbm = W1_words[g].rearrange("p n t -> p (n t)")
            pieces = 4 if g == G1 - 1 else 1
            wide = DO // pieces
            for i in range(pieces):
                nc.sync.dma_start(
                    out=w[:, wide * i : wide * (i + 1)].bitcast(I32),
                    in_=w_hbm[:, 4 * wide * i : 4 * wide * (i + 1)].bitcast(I32),
                )
            w1.append(w)
        lab_sb = keep.tile([P, DO], BF16, name="lab_sb")
        nc.sync.dma_start(out=lab_sb[:, 0:512], in_=label_vecs[:, 0:512])
        w2 = []
        w2_view = W2_words.rearrange("g p n t -> p g (n t)")
        for cg in range(NCG):
            w = keep.tile([P, G2, 512], U32, name="w2_%d" % cg, align_bytes=64)
            nc.sync.dma_start(
                out=w[:].bitcast(I32), in_=w2_view[:, :, 2048 * cg : 2048 * (cg + 1)].bitcast(I32)
            )
            w2.append(w)
            if cg == 0:
                nc.sync.dma_start(out=lab_sb[:, 512:DO], in_=label_vecs[:, 512:DO])

        bp = bank("bp", (P, 1024), BF16)
        nc.tensor.transpose(bp[:, 0:P], zt[:], ident_b[:])
        b2_t = keep.tile([P, 16], F32, name="b2_t")
        nc.vector.tensor_copy(out=b2_t[:], in_=bp[:, 0:16])
        b1_t = keep.tile([P, 16], BF16, name="b1_t")
        nc.vector.tensor_copy(out=b1_t[:], in_=bp[:, 16:32])
        b1b = keep.tile([P, DO], BF16, name="b1b")

        def spread_b1():
            for i in range(2):
                bb = bank("bb%d" % i, (P, 8, P), BF16)
                for cc in range(8):
                    c = 8 * i + cc
                    nc.tensor.transpose(bb[:, cc, :], b1_t[:, c : c + 1].to_broadcast([P, P]), ident_b[:])
                nc.scalar.copy(out=b1b[:, 1024 * i : 1024 * (i + 1)], in_=bb[:].rearrange("p c n -> p (c n)"))

        gx = keep.tile([P, G1, B, 4], BF16, name="gx", align_bytes=64)
        xq = keep.tile([P, G1, B], U32, name="xq", align_bytes=64)
        xs = keep.tile([P, G1, B], U8, name="xs", align_bytes=64)
        for h in range(2):
            nc.vector.tensor_scalar_max(
                out=x_sb[:, DH * h : DH * (h + 1)], in0=x_sb[:, DH * h : DH * (h + 1)], scalar1=0.0
            )
        x_words = x_sb[:].bitcast(F32)
        gx_words = gx[:].bitcast(F32)
        for i in range(4):
            xt = bank("xt%d" % i, (P, 2, 2, B))
            for gg in range(2):
                g = 2 * i + gg
                for u in range(2):
                    nc.tensor.transpose(
                        xt[:, gg, u, :], x_words[:, 256 * g + u : 256 * (g + 1) : 2], ident_f[:]
                    )
            src = xt[:].rearrange("p g u b -> p g b u")
            if i % 2 == 0:
                nc.vector.tensor_copy(out=gx_words[:, 2 * i : 2 * i + 2], in_=src)
            else:
                nc.scalar.copy(out=gx_words[:, 2 * i : 2 * i + 2], in_=src)

        spread_b1()

        for h in range(2):
            nc.vector.quantize_mx(
                out=xq[:, 4 * h : 4 * h + 4, :].rearrange("p g b -> p (g b)").bitcast(FP8X4),
                scales=xs[:, 4 * h : 4 * h + 4, :].rearrange("p g b -> p (g b)"),
                in_=gx[:, 4 * h : 4 * h + 4].rearrange("p g b t -> p (g b t)"),
            )

        acc = [bank("acc%d" % nb) for nb in range(4)]
        for g in range(G1):
            k = 4 * (g % 4)
            pl = planes[g // 4]
            for nb in range(4):
                cols = slice(512 * nb, 512 * (nb + 1))
                nc.tensor.matmul_mx(
                    out=acc[nb][:],
                    lhsT=xq[:, g, :].bitcast(FP8X4),
                    lhsT_scale=xs[:, g, :],
                    rhs=w1[g][:, cols].bitcast(FP8X4),
                    rhs_scale=pl[k:P, cols],
                    start=(g == 0),
                    stop=(g == G1 - 1),
                )

        h32 = keep.tile([P, DO], F32, name="h32")
        hb = keep.tile([P, DO], BF16, name="hb")
        gh = keep.tile([P, G2, B, 4], BF16, name="gh", align_bytes=64)
        hq = keep.tile([P, G2, B], U32, name="hq", align_bytes=64)
        hs = keep.tile([P, G2, B], U8, name="hs", align_bytes=64)
        for g in range(G2):
            cols = slice(512 * g, 512 * (g + 1))
            nc.vector.tensor_tensor(out=h32[:, cols], in0=acc[g][:], in1=b1b[:, cols], op=ALU.add)
            nc.scalar.activation(out=hb[:, cols], in_=h32[:, cols], func=ACT.Relu)

        def quantize_hidden(g):
            nc.vector.quantize_mx(
                out=hq[:, g, :].bitcast(FP8X4), scales=hs[:, g, :], in_=gh[:, g].rearrange("p b t -> p (b t)")
            )

        for g in range(G2):
            ht = bank("ht%d" % g, (P, 8, B), BF16)
            for t in range(4):
                nc.tensor.transpose(ht[:, t, :], hb[:, 512 * g + t : 512 * (g + 1) : 4], ident_b[:])
            src = ht[:, 0:4, :].rearrange("p t b -> p b t")
            if g % 2 == 0:
                nc.vector.tensor_copy(out=gh[:, g], in_=src)
            else:
                nc.scalar.copy(out=gh[:, g], in_=src)
            if g == 0:
                quantize_hidden(0)
            elif g == 2:
                quantize_hidden(1)
                quantize_hidden(2)
            elif g == 3:
                quantize_hidden(3)

        def turn_labels(cg):
            lp = bank("lab%d" % cg, (P, 4, L))
            for j in range(4):
                c = 4 * cg + j
                nc.tensor.matmul(
                    out=lp[:, j, :], lhsT=lab_sb[:, P * c : P * (c + 1)], rhs=ident_b[:], start=True, stop=True
                )
            return lp

        lab_next = turn_labels(0)

        emb = [keep.tile([P, 4, B], F32, name="emb%d" % cg) for cg in range(NCG)]

        def layer2(cg, own_banks):
            if own_banks:
                eps = [bank("ep%d_%d" % (cg, j))[:, 0:P] for j in range(4)]
                order = [(j, g) for g in range(G2) for j in range(4)]
            else:
                ep = bank("ep%d" % cg)
                eps = [ep[:, P * j : P * (j + 1)] for j in range(4)]
                order = [(j, g) for j in range(4) for g in range(G2)]
            for j, g in order:
                cols = slice(P * j, P * (j + 1))
                nc.tensor.matmul_mx(
                    out=eps[j],
                    lhsT=w2[cg][:, g, cols].bitcast(FP8X4),
                    lhsT_scale=planes[2][4 * g : P, 512 * cg + P * j : 512 * cg + P * (j + 1)],
                    rhs=hq[:, g, :].bitcast(FP8X4),
                    rhs_scale=hs[:, g, :],
                    start=(g == 0),
                    stop=(g == G2 - 1),
                )
            for j in range(4):
                c = 4 * cg + j
                nc.scalar.activation(
                    out=emb[cg][:, j, :], in_=eps[j], func=ACT.Identity, bias=b2_t[:, c : c + 1], scale=1.0
                )

        stats = keep.tile([P, NCG, NV, 6], F32, name="stats")
        pending = []

        def sum_squares(cg, l, tp):
            if l % V_MOD in V_RES and l // V_MOD < NVB:
                v = len(V_RES) * (l // V_MOD) + V_RES.index(l % V_MOD)
                nc.vector.bn_stats(out=stats[:, cg, v, :], in_=tp[:])
            else:
                junk = jpool.tile([P, 512], F32, name="junk", tag="junk")
                nc.scalar.activation(
                    out=junk[:], in_=tp[:], func=ACT.Square, accum_out=acc_s[:, cg, l : l + 1]
                )

        tot = keep.tile([P, L], F32, name="tot")
        tot_v = tot[:, 0 : V_MOD * NVB].rearrange("p (v f) -> p v f", f=V_MOD)[:, :, V_RES[0] : V_MOD : V_RES[1] - V_RES[0]]

        def vector_sum_steps(c0, c1):
            st = stats[:, c0:c1].rearrange("p c v (e s) -> p c v e s", s=3)
            msq = keep.tile([P, c1 - c0, NV, 2], F32, name="msq%d" % c0)
            ssq = keep.tile([P, c1 - c0, NV, 2], F32, name="ssq%d" % c0)
            sum_v = keep.tile([P, NV], F32, name="sum_v%d" % c0)
            return [
                lambda: nc.vector.tensor_tensor(
                    out=msq[:], in0=st[:, :, :, :, 1], in1=st[:, :, :, :, 1], op=ALU.mult
                ),
                lambda: nc.vector.scalar_tensor_tensor(
                    out=ssq[:], in0=msq[:], scalar=256.0, in1=st[:, :, :, :, 2], op0=ALU.mult, op1=ALU.add
                ),
                lambda: nc.vector.tensor_reduce(
                    out=sum_v[:], in_=ssq[:].rearrange("p c v e -> p v c e"), axis=AX.XY, op=ALU.add
                ),
                lambda: nc.vector.tensor_tensor(
                    out=tot_v, in0=tot_v, in1=sum_v[:].rearrange("p (v k) -> p v k", k=len(V_RES)), op=ALU.add
                ),
            ]

        early = [
            lambda: nc.vector.tensor_reduce(
                out=tot[:], in_=acc_s[:, 0 : NCG - 1, :].rearrange("p c l -> p l c"), axis=AX.X, op=ALU.add
            )
        ] + vector_sum_steps(0, NCG - 1)

        layer2(0, True)
        for cg in range(NCG):
            lab_t = lab_next
            for l in range(L):
                r = rpool.tile([P, 4, B], F32, name="r", tag="r")
                for j in range(4):
                    nc.vector.tensor_scalar(
                        out=r[:, j, :],
                        in0=emb[cg][:, j, :],
                        scalar1=lab_t[:, j, l : l + 1],
                        scalar2=0.0,
                        op0=ALU.subtract,
                        op1=ALU.min,
                    )
                tp = bank("tp")
                if l % KEEP_EVERY == 0:
                    nc.tensor.matmul_mx(
                        out=tp[:],
                        lhsT=hq[:, 0, :].bitcast(FP8X4),
                        lhsT_scale=hs[:, 0, :],
                        rhs=w1[0][:, 0:512].bitcast(FP8X4),
                        rhs_scale=planes[0][0:P, 0:512],
                        start=True,
                        stop=True,
                    )
                for j in range(4):
                    nc.tensor.transpose(tp[:, P * j : P * (j + 1)], r[:, j, :], ident_f[:])
                pending.append((cg, l, tp))
                if len(pending) > LAG:
                    sum_squares(*pending.pop(0))
                if l == 64 and cg + 1 < NCG:
                    layer2(cg + 1, False)
                if l == 96 and cg + 1 < NCG:
                    lab_next = turn_labels(cg + 1)
                if cg == NCG - 1 and l >= 4 * LAG and early:
                    early.pop(0)()
        for item in pending:
            sum_squares(*item)

        for step in vector_sum_steps(NCG - 1, NCG):
            step()
        nc.vector.tensor_tensor(out=tot[:], in0=tot[:], in1=acc_s[:, NCG - 1, :], op=ALU.add)
        root = keep.tile([P, L], F32, name="root")
        nc.scalar.activation(out=root[:], in_=tot[:], func=ACT.Sqrt)
        res = keep.tile([P, L], F32, name="res")
        nc.scalar.mul(out=res[:], in_=root[:], mul=-1.0)
        nc.sync.dma_start(out=out[:, :], in_=res[:])
